import numpy as np
import ml_dtypes


def mxq(x, axis, fmt="e4m3"):
    dtype, down = {"e4m3": (ml_dtypes.float8_e4m3fn, 7), "e5m2": (ml_dtypes.float8_e5m2, 14)}[fmt]
    v = np.moveaxis(np.asarray(x, np.float32).astype(ml_dtypes.bfloat16).astype(np.float64), axis, -1)
    blocks = v.reshape(v.shape[:-1] + (-1, 32))
    amax = np.abs(blocks).max(-1, keepdims=True)
    byte = np.maximum(np.where(amax > 0, np.frexp(amax)[1] - 1 + 127, 0) - down, 1)
    scale = np.exp2(byte - 127.0)
    codes = (blocks / scale).astype(np.float32).astype(dtype).astype(np.float64)
    return np.moveaxis((codes * scale).reshape(v.shape), -1, axis)


WIDE = False


def mx_kscale(k):
    if not WIDE:
        return np.ones(k)
    levels = np.array([10, -10, 5, -5, 0])
    if k % 512:
        return np.exp2(np.random.permutation(np.resize(levels, k // 32))).repeat(32)
    a = np.empty((k // 512, 16))
    for p in range(k // 512):
        a[p, :8] = np.random.permutation(np.resize(levels, 8))
        for g in range(8):
            far = levels[np.abs(levels - a[p, g]) >= 10]
            a[p, g + 8] = far[np.random.randint(len(far))]
    return np.exp2(a.ravel()).repeat(32)


BF16 = ml_dtypes.bfloat16


def bf(x):
    return np.asarray(x, np.float32).astype(BF16)


def f64(x):
    return np.asarray(x).astype(np.float64)


E2M1 = np.array([0.0, 0.5, 1.0, 1.5, 2.0, 3.0, 4.0, 6.0, -0.0, -0.5, -1.0, -1.5, -2.0, -3.0, -4.0, -6.0])


def pack_weight(w, fmt):
    k, n = w.shape
    w = f64(bf(w)).reshape(k // 32, 32, n)
    amax = np.abs(w).max(1)
    if fmt == "e4m3":
        byte = np.frexp(amax)[1] - 1 + 127 - 7
    else:
        mant, ex = np.frexp(amax / 6.0)
        byte = np.where(mant > 0.5, ex, ex - 1) + 127
    byte = np.clip(np.where(amax > 0, byte, 1), 1, 254)
    scaled = (w * np.exp2(127.0 - byte)[:, None, :]).reshape(k, n).astype(np.float32)
    by_word = np.ascontiguousarray(scaled.reshape(k // 512, 128, 4, n).transpose(0, 1, 3, 2))
    if fmt == "e4m3":
        words = by_word.astype(ml_dtypes.float8_e4m3fn).view(np.uint8)
    else:
        c = by_word.astype(ml_dtypes.float4_e2m1fn).view(np.uint8) & 0xF
        words = c[..., 0::2] | (c[..., 1::2] << 4)
    return np.ascontiguousarray(words), np.ascontiguousarray(byte.astype(np.uint8).reshape(k // 512, 16, n))


def unpack_weight(words, scales, fmt):
    g, p, n, _ = words.shape
    if fmt == "e4m3":
        vals = np.ascontiguousarray(words).view(ml_dtypes.float8_e4m3fn).astype(np.float64)
    else:
        nib = np.empty((g, p, n, 4), np.uint8)
        nib[..., 0::2] = words & 0xF
        nib[..., 1::2] = words >> 4
        vals = E2M1[nib]
    vals = vals * np.repeat(np.exp2(scales.astype(np.float64) - 127.0), 8, axis=1)[..., None]
    return vals.transpose(0, 1, 3, 2).reshape(g * 512, n)
def pack4(w):
    words, scales = pack_weight(w, "e2m1")
    return words.reshape(words.shape[0], 128, -1), scales


def unpack4(words, scales):
    return unpack_weight(words.reshape(words.shape[0], 128, -1, 2), scales, "e2m1")


B, A, S, F = 512, 16, 256, 512


def draw0():
    s, u = mx_kscale(F), mx_kscale(F)
    t, v = mx_kscale(F), mx_kscale(F)
    h1 = bf(np.maximum(np.random.standard_normal((B, A, F)) * 1.4, 0.0) * s)
    W2 = bf(np.random.standard_normal((A, F, F)) * 1.4 / np.sqrt(F) / s[:, None] * t)
    b2 = bf(np.random.standard_normal((A, F)) * 0.2 * t)
    W3 = bf(np.random.standard_normal((A, F, S)) / np.sqrt(F) / t[:, None])
    b3 = bf(np.random.standard_normal((A, S)) * 0.2)
    g1 = bf(np.maximum(np.random.standard_normal((B, F)) * 1.4, 0.0) * u)
    V2_words, V2_scales = pack4(np.random.standard_normal((F, F)) * 1.4 / np.sqrt(F) / u[:, None] * v)
    c2 = bf(np.random.standard_normal(F) * 0.2 * v)
    V3_words, V3_scales = pack4(np.random.standard_normal((F, S)) / np.sqrt(F) / v[:, None])
    c3 = bf(np.random.standard_normal(S) * 0.2)
    return {
        "h1": h1,
        "W2": W2,
        "b2": b2,
        "W3": W3,
        "b3": b3,
        "g1": g1,
        "V2_words": V2_words,
        "V2_scales": V2_scales,
        "c2": c2,
        "V3_words": V3_words,
        "V3_scales": V3_scales,
        "c3": c3,
    }


def core(h1, W2, b2, W3, b3, g1, V2_words, V2_scales, c2, V3_words, V3_scales, c3):
    ha = mxq(f64(h1), 2, "e4m3").transpose(1, 0, 2)
    h2 = np.maximum((ha @ mxq(f64(W2), 1, "e4m3")) + f64(b2)[:, None, :], 0.0)
    psi_adv = ((mxq(h2, 2, "e4m3") @ mxq(f64(W3), 1, "e4m3")) + f64(b3)[:, None, :]).transpose(1, 0, 2)
    g2 = np.maximum((mxq(f64(g1), 1, "e4m3") @ unpack4(V2_words, V2_scales)) + f64(c2), 0.0)
    psi_state = (mxq(g2, 1, "e4m3") @ unpack4(V3_words, V3_scales)) + f64(c3)
    return psi_state[:, None, :] + psi_adv - psi_adv.mean(axis=1, keepdims=True)


def e4m3fn_bytes(y):
    return np.clip(np.asarray(y, np.float64), -448.0, 448.0).astype(np.float32).astype(ml_dtypes.float8_e4m3fn).view(np.uint8)


def e4m3fn_values(b):
    return np.asarray(b, np.uint8).view(ml_dtypes.float8_e4m3fn).astype(np.float64)


def setup_inputs():
    d = draw0()
    x0 = np.asarray(d['h1']).astype(np.float64)
    s = (np.max(np.abs(x0), axis=(0, 1), keepdims=True) / 448.0).astype(np.float32)
    out = {}
    for k, v in d.items():
        if k == 'h1':
            out['h1_bytes'] = e4m3fn_bytes(x0 / s.astype(np.float64))
            out['h1_scale'] = s
        else:
            out[k] = v
    return out


def reference(h1_bytes, h1_scale, W2, b2, W3, b3, g1, V2_words, V2_scales, c2, V3_words, V3_scales, c3):
    return core(e4m3fn_values(h1_bytes) * h1_scale.astype(np.float64), W2, b2, W3, b3, g1, V2_words, V2_scales, c2, V3_words, V3_scales, c3)

@@ -1,0 +1,360 @@
+from contextlib import ExitStack
+
+import concourse.mybir as mybir
+from concourse.masks import make_identity
+
+B, A, S, F = 512, 16, 256, 512
+FLOPS = 2 * B * (A + 1) * (F * F + F * S)
+
+P = 128
+PACK = 4
+TOK_TILES = B // P
+S_HALVES = S // P
+
+F32 = mybir.dt.float32
+BF16 = mybir.dt.bfloat16
+I32 = mybir.dt.int32
+U32 = mybir.dt.uint32
+U8 = mybir.dt.uint8
+FP8 = mybir.dt.float8_e4m3fn
+E4M3X4 = mybir.dt.float8_e4m3fn_x4
+E2M1X4 = mybir.dt.float4_e2m1fn_x4
+ADD = mybir.AluOpType.add
+MULT = mybir.AluOpType.mult
+RELU = mybir.ActivationFunctionType.Relu
+IDENTITY = mybir.ActivationFunctionType.Identity
+AXIS_X = mybir.AxisListType.X
+
+STATE = -1
+B2, B3 = 0, 4
+C_COL = A
+
+
+def tile_psicritic_pa_w4_kernel(
+    tc, h1_bytes, h1_scale, W2, b2, W3, b3, g1, V2_words, V2_scales, c2, V3_words, V3_scales, c3, out
+):
+    nc = tc.nc
+    with ExitStack() as ctx:
+        keep = ctx.enter_context(tc.tile_pool(name="keep", bufs=1))
+        loads = ctx.enter_context(tc.tile_pool(name="loads", bufs=4))
+        work = ctx.enter_context(tc.tile_pool(name="work", bufs=2))
+        outs = ctx.enter_context(tc.tile_pool(name="outs", bufs=3))
+        psum_sum = ctx.enter_context(tc.psum_pool(name="psum_sum", bufs=1))
+        psum_t = ctx.enter_context(tc.psum_pool(name="psum_t", bufs=2))
+        psum_m = ctx.enter_context(tc.psum_pool(name="psum_m", bufs=4))
+        ctx.enter_context(tc.manual_schedule())
+
+        rows = keep.tile([P, F + S], BF16, name="rows", align_bytes=64)
+        v2_raw_s = keep.tile([P, F], U8, name="v2_raw_s", align_bytes=64)
+        v3_s = keep.tile([P, S], U8, name="v3_s", align_bytes=64)
+        v2_raw = keep.tile([P, 2 * F], U8, name="v2_raw", align_bytes=64)
+        v3_w = keep.tile([P, 2 * S], U8, name="v3_w", align_bytes=64)
+        v2_w = keep.tile([P, 2 * F], U8, name="v2_w", align_bytes=64)
+        v2_s = keep.tile([P, F], U8, name="v2_s", align_bytes=64)
+        scale = keep.tile([P, 2 * F], F32, name="scale", align_bytes=64)
+        ident_f32 = keep.tile([P, P], F32, name="ident_f32", align_bytes=64)
+        ident_bf16 = keep.tile([P, P], BF16, name="ident_bf16", align_bytes=64)
+        g1_rows = keep.tile([P, TOK_TILES, F], BF16, name="g1_rows", align_bytes=64)
+        bias = keep.tile([P, 6, 32], F32, name="bias", align_bytes=64)
+        b3_sum = keep.tile([P, S_HALVES], F32, name="b3_sum", align_bytes=64)
+        c3_mean = keep.tile([P, S_HALVES], F32, name="c3_mean", align_bytes=64)
+        state = keep.tile([P, S_HALVES, B], F32, name="state", align_bytes=64)
+        base = keep.tile([P, S_HALVES, B], F32, name="base", align_bytes=64)
+
+        hb, w2r, w3r, hs, hps, hg, hq, w2g, w2q, w3g, w3q = {}, {}, {}, {}, {}, {}, {}, {}, {}, {}, {}
+        pm, hp, h2g, h2q, sums = {}, {}, {}, {}, {}
+
+        def load(a):
+            hb[a] = loads.tile([P, TOK_TILES, F], U8, name="h_bytes", align_bytes=64)
+            nc.sync.dma_start(out=hb[a][:], in_=h1_bytes[:, a, :].rearrange("(i p) k -> p i k", p=P))
+            w2r[a] = loads.tile([P, PACK, F], BF16, name="w2_rows", align_bytes=64)
+            nc.sync.dma_start(out=w2r[a][:], in_=W2[a].rearrange("(p j) n -> p j n", j=PACK))
+            w3r[a] = loads.tile([P, PACK, S], BF16, name="w3_rows", align_bytes=64)
+            nc.sync.dma_start(out=w3r[a][:], in_=W3[a].rearrange("(p j) n -> p j n", j=PACK))
+
+        def widen(a, half):
+            if half == 0:
+                hs[a] = work.tile([P, TOK_TILES, F], BF16, name="h_rows", align_bytes=64)
+            i = slice(2 * half, 2 * half + 2)
+            nc.vector.tensor_tensor(
+                out=hs[a][:, i, :].rearrange("p i k -> p (i k)"),
+                in0=hb[a][:, i, :].rearrange("p i k -> p (i k)").bitcast(FP8),
+                in1=scale[:],
+                op=MULT,
+            )
+
+        def turn(a, half):
+            hps[a, half] = psum_t.tile([P, 2, 2, P], F32, name="turned")
+            for i in range(2):
+                words = hs[a][:, 2 * half + i, :].bitcast(F32)
+                for u in range(2):
+                    nc.tensor.transpose(hps[a, half][:, i, u, :], words[:, u::2], ident_f32[:])
+
+        def gather(a, half):
+            if half == 0:
+                hg[a] = work.tile([P, B * PACK], BF16, name="h_grouped", align_bytes=64)
+            n = B * PACK // 2
+            nc.scalar.copy(
+                out=hg[a][:, half * n : (half + 1) * n].bitcast(F32).rearrange("p (i r u) -> p i r u", i=2, u=2),
+                in_=hps[a, half][:].rearrange("p i u r -> p i r u"),
+            )
+
+        def quantize(pool, name, grouped, width):
+            codes = pool.tile([P, width], U32, name=name + "_codes", align_bytes=64)
+            scales = pool.tile([P, width], U8, name=name + "_scales", align_bytes=64)
+            nc.vector.quantize_mx(out=codes[:].bitcast(E4M3X4), scales=scales[:], in_=grouped[:])
+            return codes, scales
+
+        def quantize_h(a):
+            hq[a] = quantize(work, "h", hg[a], B)
+
+        def group_w2(a, part):
+            if part == 0:
+                w2g[a] = work.tile([P, F * PACK], BF16, name="w2_grouped", align_bytes=64)
+            m = slice(part * P // 2, (part + 1) * P // 2)
+            nc.scalar.copy(
+                out=w2g[a][:].rearrange("p (t m j) -> p m j t", t=PACK, j=PACK)[:, m],
+                in_=w2r[a][:].rearrange("p j (m t) -> p m j t", t=PACK)[:, m],
+            )
+
+        def quantize_w2(a):
+            w2q[a] = quantize(work, "w2", w2g[a], F)
+
+        def group_w3(a):
+            w3g[a] = work.tile([P, S * PACK], BF16, name="w3_grouped", align_bytes=64)
+            nc.vector.tensor_copy(
+                out=w3g[a][:].rearrange("p (c i j) -> p c j i", i=4, j=PACK),
+                in_=w3r[a][:].rearrange("p j (c i) -> p c j i", i=4),
+            )
+
+        def quantize_w3(a):
+            w3q[a] = quantize(keep, "w3_%d" % a, w3g[a], S)
+
+        def multiply1(a):
+            for t in range(PACK):
+                pm[a, t] = psum_m.tile([P, B], F32, name="products")
+                cols = slice(t * P, (t + 1) * P)
+                if a == STATE:
+                    lhsT = v2_w[:, 2 * t * P : 2 * (t + 1) * P].bitcast(E2M1X4)
+                    lhsT_scale = v2_s[:, cols]
+                else:
+                    lhsT = w2q[a][0][:, cols].bitcast(E4M3X4)
+                    lhsT_scale = w2q[a][1][:, cols]
+                nc.tensor.matmul_mx(
+                    out=pm[a, t][:],
+                    lhsT=lhsT,
+                    lhsT_scale=lhsT_scale,
+                    rhs=hq[a][0][:].bitcast(E4M3X4),
+                    rhs_scale=hq[a][1][:],
+                    start=True,
+                    stop=True,
+                )
+
+        def relu(a):
+            hp[a] = work.tile([P, PACK, B], BF16, name="h2_planes", align_bytes=64)
+            col = C_COL if a == STATE else a
+            for t in range(PACK):
+                nc.scalar.activation(
+                    out=hp[a][:, t, :], in_=pm[a, t][:], func=RELU, bias=bias[:, B2 + t, col : col + 1]
+                )
+
+        def group_h2(a):
+            h2g[a] = work.tile([P, B * PACK], BF16, name="h2_grouped", align_bytes=64)
+            nc.vector.tensor_copy(
+                out=h2g[a][:].rearrange("p (c i t) -> p c t i", i=4, t=PACK),
+                in_=hp[a][:].rearrange("p t (c i) -> p c t i", i=4),
+            )
+
+        def quantize_h2(a):
+            h2q[a] = quantize(keep, "g2" if a == STATE else "h2_%d" % a, h2g[a], B)
+
+        def multiply2(a, out_tile, half, start, stop):
+            cols = slice(half * P, (half + 1) * P)
+            if a == STATE:
+                lhsT = v3_w[:, 2 * half * P : 2 * (half + 1) * P].bitcast(E2M1X4)
+                lhsT_scale = v3_s[:, cols]
+            else:
+                lhsT = w3q[a][0][:, cols].bitcast(E4M3X4)
+                lhsT_scale = w3q[a][1][:, cols]
+            nc.tensor.matmul_mx(
+                out=out_tile[:],
+                lhsT=lhsT,
+                lhsT_scale=lhsT_scale,
+                rhs=h2q[a][0][:].bitcast(E4M3X4),
+                rhs_scale=h2q[a][1][:],
+                start=start,
+                stop=stop,
+            )
+
+        def add_to_sums(a):
+            for half in range(S_HALVES):
+                if a == 0:
+                    sums[half] = psum_sum.tile([P, B], F32, name="sum_%d" % half)
+                multiply2(a, sums[half], half, a == 0, a == A - 1)
+
+        nc.scalar.dma_start(out=scale[:, 0:F], in_=h1_scale.rearrange("o q k -> (o q k)").partition_broadcast(P))
+        g1_view = g1.rearrange("(i p) k -> p i k", p=P)
+        for half in range(2):
+            nc.sync.dma_start(out=g1_rows[:, 2 * half : 2 * half + 2, :], in_=g1_view[:, 2 * half : 2 * half + 2, :])
+        nc.vector.memset(rows[:].bitcast(I32), 0)
+        nc.vector.memset(v2_raw_s[:].bitcast(I32), 0)
+        nc.vector.memset(v3_s[:].bitcast(I32), 0)
+        make_identity(nc, ident_f32[:])
+        nc.vector.tensor_copy(out=ident_bf16[:], in_=ident_f32[:])
+        nc.scalar.dma_start(out=rows[0:A, 0:F], in_=b2)
+        nc.scalar.dma_start(out=rows[0:A, F : F + S], in_=b3)
+        nc.scalar.dma_start(out=rows[A : A + 1, 0:F], in_=c2.unsqueeze(0))
+        nc.scalar.dma_start(out=rows[A : A + 1, F : F + S], in_=c3.unsqueeze(0))
+        nc.sync.dma_start(out=v2_raw[:], in_=V2_words[0])
+        for r in range(4):
+            nc.sync.dma_start(out=v2_raw_s[r:P:32, :].bitcast(I32), in_=V2_scales[0, r:16:4, :].bitcast(I32))
+        load(0)
+        nc.sync.dma_start(out=v3_w[:], in_=V3_words[0])
+        for r in range(4):
+            nc.sync.dma_start(out=v3_s[r:P:32, :].bitcast(I32), in_=V3_scales[0, r:16:4, :].bitcast(I32))
+        load(1)
+        load(2)
+
+        hs[STATE] = g1_rows
+        turn(STATE, 0)
+        turn(STATE, 1)
+        gather(STATE, 0)
+        gather(STATE, 1)
+        turned_rows = psum_t.tile([P, 6, P], BF16, name="turned")
+        for t in range(PACK):
+            nc.tensor.transpose(turned_rows[:, B2 + t, :], rows[:, t:F:PACK], ident_bf16[:])
+        for half in range(S_HALVES):
+            nc.tensor.transpose(
+                turned_rows[:, B3 + half, :], rows[:, F + half * P : F + (half + 1) * P], ident_bf16[:]
+            )
+        nc.vector.tensor_copy(
+            out=v2_w[:].rearrange("p (t m b) -> p m t b", t=PACK, b=2),
+            in_=v2_raw[:].rearrange("p (m t b) -> p m t b", t=PACK, b=2),
+        )
+        nc.vector.tensor_copy(
+            out=v2_s[:].rearrange("p (t m) -> p m t", t=PACK), in_=v2_raw_s[:].rearrange("p (m t) -> p m t", t=PACK)
+        )
+        nc.vector.tensor_copy(out=bias[:], in_=turned_rows[:, :, 0:32])
+        quantize_h(STATE)
+        multiply1(STATE)
+        nc.scalar.copy(out=scale[:, F : 2 * F], in_=scale[:, 0:F])
+        widen(0, 0)
+        widen(0, 1)
+        turn(0, 0)
+        turn(0, 1)
+        nc.vector.tensor_reduce(out=b3_sum[:], in_=bias[:, B3 : B3 + S_HALVES, 0:A], op=ADD, axis=AXIS_X)
+        group_w3(0)
+        nc.vector.scalar_tensor_tensor(
+            out=c3_mean[:],
+            in0=b3_sum[:],
+            scalar=-1.0 / A,
+            in1=bias[:, B3 : B3 + S_HALVES, C_COL],
+            op0=MULT,
+            op1=ADD,
+        )
+        group_w2(0, 0)
+        group_w2(0, 1)
+        gather(0, 0)
+        gather(0, 1)
+        quantize_w3(0)
+
+        for a in range(A):
+            if a + 3 < A:
+                load(a + 3)
+            more = a + 1 < A
+            relu(a - 1)
+            if a == 1:
+                for half in range(S_HALVES):
+                    nc.scalar.activation(
+                        out=state[:, half, :],
+                        in_=pm[STATE, "state", half][:],
+                        func=IDENTITY,
+                        bias=c3_mean[:, half : half + 1],
+                    )
+            if more:
+                widen(a + 1, 0)
+                turn(a + 1, 0)
+                widen(a + 1, 1)
+                turn(a + 1, 1)
+                group_w3(a + 1)
+                group_w2(a + 1, 0)
+                gather(a + 1, 0)
+                gather(a + 1, 1)
+                group_w2(a + 1, 1)
+            group_h2(a - 1)
+            quantize_h(a)
+            quantize_w2(a)
+            multiply1(a)
+            quantize_h2(a - 1)
+            if more:
+                quantize_w3(a + 1)
+            if a == 0:
+                for half in range(S_HALVES):
+                    pm[STATE, "state", half] = psum_m.tile([P, B], F32, name="products")
+                    multiply2(STATE, pm[STATE, "state", half], half, True, True)
+            else:
+                add_to_sums(a - 1)
+
+        last = A - 1
+        relu(last)
+        group_h2(last)
+        quantize_h2(last)
+
+        adv, xs, turned_x, out_rows = {}, {}, {}, {}
+
+        def multiply_out(a):
+            for half in range(S_HALVES):
+                adv[a, half] = psum_m.tile([P, B], F32, name="products")
+                multiply2(a, adv[a, half], half, True, True)
+
+        def combine(a):
+            xs[a] = outs.tile([P, S_HALVES, B], F32, name="combined", align_bytes=64)
+            for half in range(S_HALVES):
+                nc.vector.scalar_tensor_tensor(
+                    out=xs[a][:, half, :],
+                    in0=adv[a, half][:],
+                    scalar=bias[:, B3 + half, a : a + 1],
+                    in1=base[:, half, :],
+                    op0=ADD,
+                    op1=ADD,
+                )
+
+        def turn_back(a):
+            for pair in range(2):
+                if pair == 0:
+                    t = psum_t.tile([P, 2, S], F32, name="turned")
+                else:
+                    t = psum_sum.tile([P, 2, S], F32, name="sum_%d" % (a % 2))
+                turned_x[a, pair] = t
+                for i in range(2):
+                    tok = slice((2 * pair + i) * P, (2 * pair + i + 1) * P)
+                    for half in range(S_HALVES):
+                        nc.tensor.transpose(
+                            t[:, i, half * P : (half + 1) * P], xs[a][:, half, tok], ident_f32[:]
+                        )
+
+        def copy_out(a):
+            if a % 2 == 0:
+                out_rows[a] = outs.tile([P, TOK_TILES, 2, S], F32, name="out_rows", align_bytes=64)
+            o = out_rows[a - a % 2]
+            for pair in range(2):
+                nc.scalar.copy(out=o[:, 2 * pair : 2 * pair + 2, a % 2, :], in_=turned_x[a, pair][:])
+            if a % 2 == 1:
+                nc.sync.dma_start(
+                    out=out[:, a - 1 : a + 1, :].rearrange("(i p) a s -> p i (a s)", p=P),
+                    in_=o[:].rearrange("p i a s -> p i (a s)"),
+                )
+
+        multiply_out(0)
+        add_to_sums(last)
+        multiply_out(1)
+        for half in range(S_HALVES):
+            nc.vector.scalar_tensor_tensor(
+                out=base[:, half, :], in0=sums[half][:], scalar=-1.0 / A, in1=state[:, half, :], op0=MULT, op1=ADD
+            )
+        for a in range(A):
+            combine(a)
+            turn_back(a)
+            if a + 2 < A:
+                multiply_out(a + 2)
+            copy_out(a)

@@ -21,13 +21,21 @@ E4M3X4 = mybir.dt.float8_e4m3fn_x4
 E2M1X4 = mybir.dt.float4_e2m1fn_x4
 ADD = mybir.AluOpType.add
 MULT = mybir.AluOpType.mult
+MAX = mybir.AluOpType.max
 RELU = mybir.ActivationFunctionType.Relu
 IDENTITY = mybir.ActivationFunctionType.Identity
 AXIS_X = mybir.AxisListType.X
 
-STATE = -1
+STATE = A
+ORDER = list(range(5)) + [STATE] + list(range(5, A))
 B2, B3 = 0, 4
-C_COL = A
+W2_VECTOR = 40
+W2_SPLIT = 84
+HEAD_VECTOR = 64
+ROW_FIRST = 10
+OUT_ORDER = [10, 11, 12, 0, 1, 2, 3, 13, 4, 5, 14, 6, 7, 15, 8, 9]
+STORES_AFTER = {1: [0], 2: [5], 3: [1], 5: [2], 6: [6], 7: [3], 9: [4, 7]}
+EARLY = 2
 
 
 def tile_psicritic_pa_w4_kernel(
@@ -36,9 +44,9 @@ def tile_psicritic_pa_w4_kernel(
     nc = tc.nc
     with ExitStack() as ctx:
         keep = ctx.enter_context(tc.tile_pool(name="keep", bufs=1))
-        loads = ctx.enter_context(tc.tile_pool(name="loads", bufs=4))
+        loads = ctx.enter_context(tc.tile_pool(name="loads", bufs=3))
         work = ctx.enter_context(tc.tile_pool(name="work", bufs=2))
-        outs = ctx.enter_context(tc.tile_pool(name="outs", bufs=3))
+        outs = ctx.enter_context(tc.tile_pool(name="outs", bufs=7))
         psum_sum = ctx.enter_context(tc.psum_pool(name="psum_sum", bufs=1))
         psum_t = ctx.enter_context(tc.psum_pool(name="psum_t", bufs=2))
         psum_m = ctx.enter_context(tc.psum_pool(name="psum_m", bufs=4))
@@ -55,24 +63,49 @@ def tile_psicritic_pa_w4_kernel(
         ident_f32 = keep.tile([P, P], F32, name="ident_f32", align_bytes=64)
         ident_bf16 = keep.tile([P, P], BF16, name="ident_bf16", align_bytes=64)
         g1_rows = keep.tile([P, TOK_TILES, F], BF16, name="g1_rows", align_bytes=64)
+        b3_rows = keep.tile([P, A - ROW_FIRST, S], BF16, name="b3_rows", align_bytes=64)
         bias = keep.tile([P, 6, 32], F32, name="bias", align_bytes=64)
         b3_sum = keep.tile([P, S_HALVES], F32, name="b3_sum", align_bytes=64)
         c3_mean = keep.tile([P, S_HALVES], F32, name="c3_mean", align_bytes=64)
         state = keep.tile([P, S_HALVES, B], F32, name="state", align_bytes=64)
         base = keep.tile([P, S_HALVES, B], F32, name="base", align_bytes=64)
+        base_rows = keep.tile([P, TOK_TILES, S], F32, name="base_rows", align_bytes=64)
 
-        hb, w2r, w3r, hs, hps, hg, hq, w2g, w2q, w3g, w3q = {}, {}, {}, {}, {}, {}, {}, {}, {}, {}, {}
+        hb, w2r, w3r, hs, hps, hg, hq, w2g, w2q, w3p, w3g, w3q = {}, {}, {}, {}, {}, {}, {}, {}, {}, {}, {}, {}
         pm, hp, h2g, h2q, sums = {}, {}, {}, {}, {}
 
-        def load(a):
+        def load_h(a):
             hb[a] = loads.tile([P, TOK_TILES, F], U8, name="h_bytes", align_bytes=64)
             nc.sync.dma_start(out=hb[a][:], in_=h1_bytes[:, a, :].rearrange("(i p) k -> p i k", p=P))
+
+        def load_w2(a):
             w2r[a] = loads.tile([P, PACK, F], BF16, name="w2_rows", align_bytes=64)
             nc.sync.dma_start(out=w2r[a][:], in_=W2[a].rearrange("(p j) n -> p j n", j=PACK))
+
+        def load_w3(a):
             w3r[a] = loads.tile([P, PACK, S], BF16, name="w3_rows", align_bytes=64)
             nc.sync.dma_start(out=w3r[a][:], in_=W3[a].rearrange("(p j) n -> p j n", j=PACK))
 
+        def load_state():
+            nc.sync.dma_start(out=g1_rows[:], in_=g1.rearrange("(i p) k -> p i k", p=P))
+            nc.sync.dma_start(out=v2_raw[:], in_=V2_words[0])
+            nc.sync.dma_start(out=v3_w[:], in_=V3_words[0])
+            for r in range(4):
+                nc.sync.dma_start(out=v2_raw_s[r:P:32, :].bitcast(I32), in_=V2_scales[0, r:16:4, :].bitcast(I32))
+                nc.sync.dma_start(out=v3_s[r:P:32, :].bitcast(I32), in_=V3_scales[0, r:16:4, :].bitcast(I32))
+            hs[STATE] = g1_rows
+
+        def load(a):
+            if a == STATE:
+                load_state()
+            else:
+                load_h(a)
+                load_w2(a)
+                load_w3(a)
+
         def widen(a, half):
+            if a == STATE:
+                return
             if half == 0:
                 hs[a] = work.tile([P, TOK_TILES, F], BF16, name="h_rows", align_bytes=64)
             i = slice(2 * half, 2 * half + 2)
@@ -108,27 +141,61 @@ def tile_psicritic_pa_w4_kernel(
         def quantize_h(a):
             hq[a] = quantize(work, "h", hg[a], B)
 
-        def group_w2(a, part):
-            if part == 0:
+        def group_w2(engine_copy, a, first, last):
+            if a == STATE:
+                return
+            if a not in w2g:
                 w2g[a] = work.tile([P, F * PACK], BF16, name="w2_grouped", align_bytes=64)
-            m = slice(part * P // 2, (part + 1) * P // 2)
-            nc.scalar.copy(
-                out=w2g[a][:].rearrange("p (t m j) -> p m j t", t=PACK, j=PACK)[:, m],
-                in_=w2r[a][:].rearrange("p j (m t) -> p m j t", t=PACK)[:, m],
+            m = slice(first, last)
+            engine_copy(
+                out=w2g[a][:].rearrange("p (t m j) -> p t m j", t=PACK, j=PACK)[:, :, m],
+                in_=w2r[a][:].rearrange("p j (m t) -> p t m j", t=PACK)[:, :, m],
             )
 
         def quantize_w2(a):
-            w2q[a] = quantize(work, "w2", w2g[a], F)
+            if a != STATE:
+                w2q[a] = quantize(work, "w2", w2g[a], F)
+
+        def spread_w3(a):
+            if a == STATE or a == ORDER[-1]:
+                return
+            w3p[a] = psum_t.tile([P, S, PACK], BF16, name="turned")
+            n = S // 2
+            for half in range(2):
+                cols = slice(half * n, (half + 1) * n)
+                nc.tensor.matmul(
+                    w3p[a][:, cols, :].rearrange("p n j -> p (n j)"),
+                    lhsT=ident_bf16[:],
+                    rhs=w3r[a][:, :, cols].rearrange("p j n -> p n j"),
+                    start=True,
+                    stop=True,
+                )
 
         def group_w3(a):
+            if a == STATE:
+                return
             w3g[a] = work.tile([P, S * PACK], BF16, name="w3_grouped", align_bytes=64)
-            nc.vector.tensor_copy(
-                out=w3g[a][:].rearrange("p (c i j) -> p c j i", i=4, j=PACK),
-                in_=w3r[a][:].rearrange("p j (c i) -> p c j i", i=4),
-            )
+            if a == ORDER[-1]:
+                nc.vector.tensor_copy(
+                    out=w3g[a][:].rearrange("p (c i j) -> p c j i", i=4, j=PACK),
+                    in_=w3r[a][:].rearrange("p j (c i) -> p c j i", i=4),
+                )
+            else:
+                nc.scalar.copy(out=w3g[a][:], in_=w3p[a][:].rearrange("p n j -> p (n j)"))
 
         def quantize_w3(a):
-            w3q[a] = quantize(keep, "w3_%d" % a, w3g[a], S)
+            if a != STATE:
+                w3q[a] = quantize(keep, "w3_%d" % a, w3g[a], S)
+
+        def permute_v2():
+            nc.vector.tensor_copy(
+                out=v2_w[:].rearrange("p (t m b) -> p m t b", t=PACK, b=2),
+                in_=v2_raw[:].rearrange("p (m t b) -> p m t b", t=PACK, b=2),
+            )
+            nc.vector.tensor_copy(
+                out=v2_s[:].rearrange("p (t m) -> p m t", t=PACK),
+                in_=v2_raw_s[:].rearrange("p (m t) -> p m t", t=PACK),
+            )
 
         def multiply1(a):
             for t in range(PACK):
@@ -152,11 +219,14 @@ def tile_psicritic_pa_w4_kernel(
 
         def relu(a):
             hp[a] = work.tile([P, PACK, B], BF16, name="h2_planes", align_bytes=64)
-            col = C_COL if a == STATE else a
             for t in range(PACK):
-                nc.scalar.activation(
-                    out=hp[a][:, t, :], in_=pm[a, t][:], func=RELU, bias=bias[:, B2 + t, col : col + 1]
-                )
+                column = bias[:, B2 + t, a : a + 1]
+                if a == ORDER[-1] and t % 2 == 1:
+                    nc.vector.tensor_scalar(
+                        out=hp[a][:, t, :], in0=pm[a, t][:], scalar1=column, scalar2=0.0, op0=ADD, op1=MAX
+                    )
+                else:
+                    nc.scalar.activation(out=hp[a][:, t, :], in_=pm[a, t][:], func=RELU, bias=column)
 
         def group_h2(a):
             h2g[a] = work.tile([P, B * PACK], BF16, name="h2_grouped", align_bytes=64)
@@ -166,7 +236,7 @@ def tile_psicritic_pa_w4_kernel(
             )
 
         def quantize_h2(a):
-            h2q[a] = quantize(keep, "g2" if a == STATE else "h2_%d" % a, h2g[a], B)
+            h2q[a] = quantize(keep, "h2_%d" % a, h2g[a], B)
 
         def multiply2(a, out_tile, half, start, stop):
             cols = slice(half * P, (half + 1) * P)
@@ -188,173 +258,218 @@ def tile_psicritic_pa_w4_kernel(
 
         def add_to_sums(a):
             for half in range(S_HALVES):
-                if a == 0:
-                    sums[half] = psum_sum.tile([P, B], F32, name="sum_%d" % half)
-                multiply2(a, sums[half], half, a == 0, a == A - 1)
+                if a == STATE:
+                    pm[a, "out", half] = psum_m.tile([P, B], F32, name="products")
+                    multiply2(a, pm[a, "out", half], half, True, True)
+                else:
+                    if a == 0:
+                        sums[half] = psum_sum.tile([P, B], F32, name="sum_%d" % half)
+                    multiply2(a, sums[half], half, a == 0, a == A - 1)
+
+        def keep_state():
+            for half in range(S_HALVES):
+                nc.scalar.activation(
+                    out=state[:, half, :],
+                    in_=pm[STATE, "out", half][:],
+                    func=IDENTITY,
+                    bias=c3_mean[:, half : half + 1],
+                )
+
+        adv, xs, turned_x, out_rows = {}, {}, {}, {}
+
+        def out_slot(a):
+            if a // 2 not in out_rows:
+                out_rows[a // 2] = outs.tile([P, TOK_TILES, 2, S], F32, name="out_rows", align_bytes=64)
+            return out_rows[a // 2]
+
+        def store(a, first):
+            first, last = first, first + 2
+            nc.sync.dma_start(
+                out=out[first * P : last * P, a - a % 2 : a - a % 2 + 2, :].rearrange("(i p) a s -> p i (a s)", p=P),
+                in_=out_slot(a)[:, first:last].rearrange("p i a s -> p i (a s)"),
+            )
+
+        def multiply_out(a, pool, name):
+            for part in range(2):
+                adv[a, part] = pool.tile([P, B], F32, name=name)
+                if a < ROW_FIRST:
+                    multiply2(a, adv[a, part], part, True, True)
+                else:
+                    for i in range(2):
+                        tok = slice((2 * part + i) * P, (2 * part + i + 1) * P)
+                        nc.tensor.matmul_mx(
+                            out=adv[a, part][:, i * S : (i + 1) * S],
+                            lhsT=h2q[a][0][:, tok].bitcast(E4M3X4),
+                            lhsT_scale=h2q[a][1][:, tok],
+                            rhs=w3q[a][0][:].bitcast(E4M3X4),
+                            rhs_scale=w3q[a][1][:],
+                            start=True,
+                            stop=True,
+                        )
+
+        def combine(a):
+            if a < ROW_FIRST:
+                xs[a] = work.tile([P, S_HALVES, B], F32, name="combined", align_bytes=64)
+                for half in range(S_HALVES):
+                    nc.vector.scalar_tensor_tensor(
+                        out=xs[a][:, half, :],
+                        in0=adv[a, half][:],
+                        scalar=bias[:, B3 + half, a : a + 1],
+                        in1=base[:, half, :],
+                        op0=ADD,
+                        op1=ADD,
+                    )
+            else:
+                for part in range(2):
+                    for i in range(2):
+                        nc.vector.tensor_tensor(
+                            out=out_slot(a)[:, 2 * part + i, a % 2, :],
+                            in0=adv[a, part][:, i * S : (i + 1) * S],
+                            in1=b3_rows[:, a - ROW_FIRST, :],
+                            op=ADD,
+                        )
+
+        def turn_back(a, source, n):
+            for part in range(2):
+                if part == 0:
+                    t = psum_t.tile([P, 2, S], F32, name="turned")
+                else:
+                    t = psum_sum.tile([P, 2, S], F32, name="sum_%d" % (n % 2))
+                turned_x[a, part] = t
+                for i in range(2):
+                    tok = slice((2 * part + i) * P, (2 * part + i + 1) * P)
+                    for half in range(S_HALVES):
+                        nc.tensor.transpose(t[:, i, half * P : (half + 1) * P], source[:, half, tok], ident_f32[:])
+
+        def finish(a):
+            o = out_slot(a)
+            for part in range(2):
+                if a < ROW_FIRST:
+                    nc.scalar.copy(out=o[:, 2 * part : 2 * part + 2, a % 2, :], in_=turned_x[a, part][:])
+                else:
+                    for i in (2 * part, 2 * part + 1):
+                        nc.gpsimd.tensor_tensor(
+                            out=o[:, i, a % 2, :], in0=o[:, i, a % 2, :], in1=base_rows[:, i, :], op=ADD
+                        )
 
         nc.scalar.dma_start(out=scale[:, 0:F], in_=h1_scale.rearrange("o q k -> (o q k)").partition_broadcast(P))
-        g1_view = g1.rearrange("(i p) k -> p i k", p=P)
-        for half in range(2):
-            nc.sync.dma_start(out=g1_rows[:, 2 * half : 2 * half + 2, :], in_=g1_view[:, 2 * half : 2 * half + 2, :])
+        load_w2(0)
+        load_h(0)
+        load_h(1)
+        load_w3(0)
         nc.vector.memset(rows[:].bitcast(I32), 0)
-        nc.vector.memset(v2_raw_s[:].bitcast(I32), 0)
-        nc.vector.memset(v3_s[:].bitcast(I32), 0)
         make_identity(nc, ident_f32[:])
         nc.vector.tensor_copy(out=ident_bf16[:], in_=ident_f32[:])
         nc.scalar.dma_start(out=rows[0:A, 0:F], in_=b2)
         nc.scalar.dma_start(out=rows[0:A, F : F + S], in_=b3)
         nc.scalar.dma_start(out=rows[A : A + 1, 0:F], in_=c2.unsqueeze(0))
         nc.scalar.dma_start(out=rows[A : A + 1, F : F + S], in_=c3.unsqueeze(0))
-        nc.sync.dma_start(out=v2_raw[:], in_=V2_words[0])
-        for r in range(4):
-            nc.sync.dma_start(out=v2_raw_s[r:P:32, :].bitcast(I32), in_=V2_scales[0, r:16:4, :].bitcast(I32))
-        load(0)
-        nc.sync.dma_start(out=v3_w[:], in_=V3_words[0])
-        for r in range(4):
-            nc.sync.dma_start(out=v3_s[r:P:32, :].bitcast(I32), in_=V3_scales[0, r:16:4, :].bitcast(I32))
-        load(1)
+        nc.vector.memset(v2_raw_s[:].bitcast(I32), 0)
+        nc.vector.memset(v3_s[:].bitcast(I32), 0)
+        load_w2(1)
+        load_w3(1)
         load(2)
 
-        hs[STATE] = g1_rows
-        turn(STATE, 0)
-        turn(STATE, 1)
-        gather(STATE, 0)
-        gather(STATE, 1)
-        turned_rows = psum_t.tile([P, 6, P], BF16, name="turned")
+        group_w2(nc.vector.tensor_copy, 0, 0, HEAD_VECTOR)
+        nc.scalar.copy(out=scale[:, F : 2 * F], in_=scale[:, 0:F])
+        group_w2(nc.scalar.copy, 0, HEAD_VECTOR, P)
+        widen(0, 0)
+        turn(0, 0)
+        widen(0, 1)
+        turn(0, 1)
+        turned_rows = psum_m.tile([P, 6, P], BF16, name="products")
         for t in range(PACK):
             nc.tensor.transpose(turned_rows[:, B2 + t, :], rows[:, t:F:PACK], ident_bf16[:])
         for half in range(S_HALVES):
             nc.tensor.transpose(
                 turned_rows[:, B3 + half, :], rows[:, F + half * P : F + (half + 1) * P], ident_bf16[:]
             )
-        nc.vector.tensor_copy(
-            out=v2_w[:].rearrange("p (t m b) -> p m t b", t=PACK, b=2),
-            in_=v2_raw[:].rearrange("p (m t b) -> p m t b", t=PACK, b=2),
-        )
-        nc.vector.tensor_copy(
-            out=v2_s[:].rearrange("p (t m) -> p m t", t=PACK), in_=v2_raw_s[:].rearrange("p (m t) -> p m t", t=PACK)
-        )
-        nc.vector.tensor_copy(out=bias[:], in_=turned_rows[:, :, 0:32])
-        quantize_h(STATE)
-        multiply1(STATE)
-        nc.scalar.copy(out=scale[:, F : 2 * F], in_=scale[:, 0:F])
-        widen(0, 0)
-        widen(0, 1)
-        turn(0, 0)
-        turn(0, 1)
-        nc.vector.tensor_reduce(out=b3_sum[:], in_=bias[:, B3 : B3 + S_HALVES, 0:A], op=ADD, axis=AXIS_X)
-        group_w3(0)
-        nc.vector.scalar_tensor_tensor(
-            out=c3_mean[:],
-            in0=b3_sum[:],
-            scalar=-1.0 / A,
-            in1=bias[:, B3 : B3 + S_HALVES, C_COL],
-            op0=MULT,
-            op1=ADD,
-        )
-        group_w2(0, 0)
-        group_w2(0, 1)
         gather(0, 0)
         gather(0, 1)
-        quantize_w3(0)
+        spread_w3(0)
+        group_w3(0)
 
-        for a in range(A):
-            if a + 3 < A:
-                load(a + 3)
-            more = a + 1 < A
-            relu(a - 1)
-            if a == 1:
-                for half in range(S_HALVES):
-                    nc.scalar.activation(
-                        out=state[:, half, :],
-                        in_=pm[STATE, "state", half][:],
-                        func=IDENTITY,
-                        bias=c3_mean[:, half : half + 1],
-                    )
-            if more:
-                widen(a + 1, 0)
-                turn(a + 1, 0)
-                widen(a + 1, 1)
-                turn(a + 1, 1)
-                group_w3(a + 1)
-                group_w2(a + 1, 0)
-                gather(a + 1, 0)
-                gather(a + 1, 1)
-                group_w2(a + 1, 1)
-            group_h2(a - 1)
+        for pos, a in enumerate(ORDER):
+            before = ORDER[pos - 1] if pos > 0 else None
+            after = ORDER[pos + 1] if pos + 1 < len(ORDER) else None
+            if pos + 3 < len(ORDER):
+                load(ORDER[pos + 3])
+            if pos + 3 == len(ORDER):
+                nc.sync.dma_start(
+                    out=b3_rows[:].rearrange("p a s -> p (a s)"),
+                    in_=b3[ROW_FIRST:A, :].rearrange("a s -> (a s)").partition_broadcast(P),
+                )
+            if before is not None:
+                relu(before)
+                group_w3(a)
+                if pos > 1 and ORDER[pos - 2] == STATE:
+                    keep_state()
+            if after is not None:
+                widen(after, 0)
+                turn(after, 0)
+                widen(after, 1)
+                turn(after, 1)
+                group_w2(nc.vector.tensor_copy, after, 0, W2_VECTOR)
+                group_w2(nc.scalar.copy, after, W2_VECTOR, W2_SPLIT)
+                gather(after, 0)
+                gather(after, 1)
+                group_w2(nc.scalar.copy, after, W2_SPLIT, P)
+            else:
+                for n in range(EARLY):
+                    multiply_out(OUT_ORDER[n], psum_t, "turned")
+                    combine(OUT_ORDER[n])
+            if after == STATE:
+                permute_v2()
+            if before is not None:
+                group_h2(before)
             quantize_h(a)
             quantize_w2(a)
             multiply1(a)
-            quantize_h2(a - 1)
-            if more:
-                quantize_w3(a + 1)
-            if a == 0:
-                for half in range(S_HALVES):
-                    pm[STATE, "state", half] = psum_m.tile([P, B], F32, name="products")
-                    multiply2(STATE, pm[STATE, "state", half], half, True, True)
-            else:
-                add_to_sums(a - 1)
+            quantize_w3(a)
+            if before is not None:
+                quantize_h2(before)
+                add_to_sums(before)
+            if after is not None:
+                spread_w3(after)
+            if pos == 0:
+                nc.vector.tensor_copy(out=bias[:], in_=turned_rows[:, :, 0:32])
+                nc.vector.tensor_reduce(out=b3_sum[:], in_=bias[:, B3 : B3 + S_HALVES, 0:A], op=ADD, axis=AXIS_X)
+            if pos == 1:
+                nc.vector.scalar_tensor_tensor(
+                    out=c3_mean[:],
+                    in0=b3_sum[:],
+                    scalar=-1.0 / A,
+                    in1=bias[:, B3 : B3 + S_HALVES, A],
+                    op0=MULT,
+                    op1=ADD,
+                )
 
         last = A - 1
         relu(last)
         group_h2(last)
         quantize_h2(last)
-
-        adv, xs, turned_x, out_rows = {}, {}, {}, {}
-
-        def multiply_out(a):
-            for half in range(S_HALVES):
-                adv[a, half] = psum_m.tile([P, B], F32, name="products")
-                multiply2(a, adv[a, half], half, True, True)
-
-        def combine(a):
-            xs[a] = outs.tile([P, S_HALVES, B], F32, name="combined", align_bytes=64)
-            for half in range(S_HALVES):
-                nc.vector.scalar_tensor_tensor(
-                    out=xs[a][:, half, :],
-                    in0=adv[a, half][:],
-                    scalar=bias[:, B3 + half, a : a + 1],
-                    in1=base[:, half, :],
-                    op0=ADD,
-                    op1=ADD,
-                )
-
-        def turn_back(a):
-            for pair in range(2):
-                if pair == 0:
-                    t = psum_t.tile([P, 2, S], F32, name="turned")
-                else:
-                    t = psum_sum.tile([P, 2, S], F32, name="sum_%d" % (a % 2))
-                turned_x[a, pair] = t
-                for i in range(2):
-                    tok = slice((2 * pair + i) * P, (2 * pair + i + 1) * P)
-                    for half in range(S_HALVES):
-                        nc.tensor.transpose(
-                            t[:, i, half * P : (half + 1) * P], xs[a][:, half, tok], ident_f32[:]
-                        )
-
-        def copy_out(a):
-            if a % 2 == 0:
-                out_rows[a] = outs.tile([P, TOK_TILES, 2, S], F32, name="out_rows", align_bytes=64)
-            o = out_rows[a - a % 2]
-            for pair in range(2):
-                nc.scalar.copy(out=o[:, 2 * pair : 2 * pair + 2, a % 2, :], in_=turned_x[a, pair][:])
-            if a % 2 == 1:
-                nc.sync.dma_start(
-                    out=out[:, a - 1 : a + 1, :].rearrange("(i p) a s -> p i (a s)", p=P),
-                    in_=o[:].rearrange("p i a s -> p i (a s)"),
-                )
-
-        multiply_out(0)
+        multiply_out(OUT_ORDER[EARLY], psum_t, "turned")
+        combine(OUT_ORDER[EARLY])
+        for a in OUT_ORDER[EARLY + 1 : EARLY + 3]:
+            multiply_out(a, psum_m, "products")
         add_to_sums(last)
-        multiply_out(1)
         for half in range(S_HALVES):
             nc.vector.scalar_tensor_tensor(
                 out=base[:, half, :], in0=sums[half][:], scalar=-1.0 / A, in1=state[:, half, :], op0=MULT, op1=ADD
             )
-        for a in range(A):
+        turn_back("base", base, 0)
+        for part in range(2):
+            nc.scalar.copy(out=base_rows[:, 2 * part : 2 * part + 2, :], in_=turned_x["base", part][:])
+        for a in OUT_ORDER[: EARLY + 1]:
+            finish(a)
+        for n in range(EARLY + 1, A):
+            a = OUT_ORDER[n]
             combine(a)
-            turn_back(a)
-            if a + 2 < A:
-                multiply_out(a + 2)
-            copy_out(a)
+            if a < ROW_FIRST:
+                turn_back(a, xs[a], n)
+            if n + 2 < A:
+                multiply_out(OUT_ORDER[n + 2], psum_m, "products")
+            finish(a)
+            for pair in STORES_AFTER.get(a, ()):
+                store(2 * pair, 0)
+                store(2 * pair, 2)

@@ -148,8 +148,8 @@ def tile_psicritic_pa_w4_kernel(
                 w2g[a] = work.tile([P, F * PACK], BF16, name="w2_grouped", align_bytes=64)
             m = slice(first, last)
             engine_copy(
-                out=w2g[a][:].rearrange("p (t m j) -> p t m j", t=PACK, j=PACK)[:, :, m],
-                in_=w2r[a][:].rearrange("p j (m t) -> p t m j", t=PACK)[:, :, m],
+                out=w2g[a][:].rearrange("p (t m j) -> p m j t", t=PACK, j=PACK)[:, m],
+                in_=w2r[a][:].rearrange("p j (m t) -> p m j t", t=PACK)[:, m],
             )
 
         def quantize_w2(a):

@@ -28,14 +28,13 @@ AXIS_X = mybir.AxisListType.X
 
 STATE = A
 ORDER = list(range(5)) + [STATE] + list(range(5, A))
+SHARED_RELU = (ORDER[ORDER.index(STATE) - 1], ORDER[-1])
 B2, B3 = 0, 4
-W2_VECTOR = 40
-W2_SPLIT = 84
-HEAD_VECTOR = 64
-ROW_FIRST = 10
-OUT_ORDER = [10, 11, 12, 0, 1, 2, 3, 13, 4, 5, 14, 6, 7, 15, 8, 9]
-STORES_AFTER = {1: [0], 2: [5], 3: [1], 5: [2], 6: [6], 7: [3], 9: [4, 7]}
-EARLY = 2
+W2_SPLIT = 64
+ROW_FIRST, ROW_COUNT = 12, 2
+BY_VECTOR = [12, 13]
+BY_SCALAR = [8, 9, 10]
+LATE = [0, 1, 11, 2, 3, 4, 5, 6, 7, 14, 15]
 
 
 def tile_psicritic_pa_w4_kernel(
@@ -63,7 +62,7 @@ def tile_psicritic_pa_w4_kernel(
         ident_f32 = keep.tile([P, P], F32, name="ident_f32", align_bytes=64)
         ident_bf16 = keep.tile([P, P], BF16, name="ident_bf16", align_bytes=64)
         g1_rows = keep.tile([P, TOK_TILES, F], BF16, name="g1_rows", align_bytes=64)
-        b3_rows = keep.tile([P, A - ROW_FIRST, S], BF16, name="b3_rows", align_bytes=64)
+        b3_rows = keep.tile([P, ROW_COUNT, S], BF16, name="b3_rows", align_bytes=64)
         bias = keep.tile([P, 6, 32], F32, name="bias", align_bytes=64)
         b3_sum = keep.tile([P, S_HALVES], F32, name="b3_sum", align_bytes=64)
         c3_mean = keep.tile([P, S_HALVES], F32, name="c3_mean", align_bytes=64)
@@ -88,10 +87,8 @@ def tile_psicritic_pa_w4_kernel(
 
         def load_state():
             nc.sync.dma_start(out=g1_rows[:], in_=g1.rearrange("(i p) k -> p i k", p=P))
-            nc.sync.dma_start(out=v2_raw[:], in_=V2_words[0])
             nc.sync.dma_start(out=v3_w[:], in_=V3_words[0])
             for r in range(4):
-                nc.sync.dma_start(out=v2_raw_s[r:P:32, :].bitcast(I32), in_=V2_scales[0, r:16:4, :].bitcast(I32))
                 nc.sync.dma_start(out=v3_s[r:P:32, :].bitcast(I32), in_=V3_scales[0, r:16:4, :].bitcast(I32))
             hs[STATE] = g1_rows
 
@@ -104,8 +101,6 @@ def tile_psicritic_pa_w4_kernel(
                 load_w3(a)
 
         def widen(a, half):
-            if a == STATE:
-                return
             if half == 0:
                 hs[a] = work.tile([P, TOK_TILES, F], BF16, name="h_rows", align_bytes=64)
             i = slice(2 * half, 2 * half + 2)
@@ -156,32 +151,14 @@ def tile_psicritic_pa_w4_kernel(
             if a != STATE:
                 w2q[a] = quantize(work, "w2", w2g[a], F)
 
-        def spread_w3(a):
-            if a == STATE or a == ORDER[-1]:
-                return
-            w3p[a] = psum_t.tile([P, S, PACK], BF16, name="turned")
-            n = S // 2
-            for half in range(2):
-                cols = slice(half * n, (half + 1) * n)
-                nc.tensor.matmul(
-                    w3p[a][:, cols, :].rearrange("p n j -> p (n j)"),
-                    lhsT=ident_bf16[:],
-                    rhs=w3r[a][:, :, cols].rearrange("p j n -> p n j"),
-                    start=True,
-                    stop=True,
-                )
-
         def group_w3(a):
             if a == STATE:
                 return
             w3g[a] = work.tile([P, S * PACK], BF16, name="w3_grouped", align_bytes=64)
-            if a == ORDER[-1]:
-                nc.vector.tensor_copy(
-                    out=w3g[a][:].rearrange("p (c i j) -> p c j i", i=4, j=PACK),
-                    in_=w3r[a][:].rearrange("p j (c i) -> p c j i", i=4),
-                )
-            else:
-                nc.scalar.copy(out=w3g[a][:], in_=w3p[a][:].rearrange("p n j -> p (n j)"))
+            nc.vector.tensor_copy(
+                out=w3g[a][:].rearrange("p (c i j) -> p c j i", i=4, j=PACK),
+                in_=w3r[a][:].rearrange("p j (c i) -> p c j i", i=4),
+            )
 
         def quantize_w3(a):
             if a != STATE:
@@ -221,7 +198,7 @@ def tile_psicritic_pa_w4_kernel(
             hp[a] = work.tile([P, PACK, B], BF16, name="h2_planes", align_bytes=64)
             for t in range(PACK):
                 column = bias[:, B2 + t, a : a + 1]
-                if a == ORDER[-1] and t % 2 == 1:
+                if a in SHARED_RELU and t % 2 == 1:
                     nc.vector.tensor_scalar(
                         out=hp[a][:, t, :], in0=pm[a, t][:], scalar1=column, scalar2=0.0, op0=ADD, op1=MAX
                     )
@@ -292,7 +269,7 @@ def tile_psicritic_pa_w4_kernel(
         def multiply_out(a, pool, name):
             for part in range(2):
                 adv[a, part] = pool.tile([P, B], F32, name=name)
-                if a < ROW_FIRST:
+                if a not in BY_VECTOR:
                     multiply2(a, adv[a, part], part, True, True)
                 else:
                     for i in range(2):
@@ -307,56 +284,70 @@ def tile_psicritic_pa_w4_kernel(
                             stop=True,
                         )
 
-        def combine(a):
-            if a < ROW_FIRST:
-                xs[a] = work.tile([P, S_HALVES, B], F32, name="combined", align_bytes=64)
-                for half in range(S_HALVES):
-                    nc.vector.scalar_tensor_tensor(
-                        out=xs[a][:, half, :],
-                        in0=adv[a, half][:],
-                        scalar=bias[:, B3 + half, a : a + 1],
-                        in1=base[:, half, :],
-                        op0=ADD,
-                        op1=ADD,
-                    )
-            else:
-                for part in range(2):
-                    for i in range(2):
-                        nc.vector.tensor_tensor(
-                            out=out_slot(a)[:, 2 * part + i, a % 2, :],
-                            in0=adv[a, part][:, i * S : (i + 1) * S],
-                            in1=b3_rows[:, a - ROW_FIRST, :],
-                            op=ADD,
-                        )
+        def add_b3_rows(a):
+            for i in range(TOK_TILES):
+                nc.vector.tensor_tensor(
+                    out=out_slot(a)[:, i, a % 2, :],
+                    in0=adv[a, i // 2][:, i % 2 * S : (i % 2 + 1) * S],
+                    in1=b3_rows[:, a - ROW_FIRST, :],
+                    op=ADD,
+                )
 
-        def turn_back(a, source, n):
+        def add_b3_columns(a):
+            xs[a] = work.tile([P, S_HALVES, B], F32, name="combined", align_bytes=64)
+            for half in range(S_HALVES):
+                nc.scalar.activation(
+                    out=xs[a][:, half, :],
+                    in_=adv[a, half][:],
+                    func=IDENTITY,
+                    bias=bias[:, B3 + half, a : a + 1],
+                )
+
+        def combine(a):
+            xs[a] = work.tile([P, S_HALVES, B], F32, name="combined", align_bytes=64)
+            for half in range(S_HALVES):
+                nc.vector.scalar_tensor_tensor(
+                    out=xs[a][:, half, :],
+                    in0=adv[a, half][:],
+                    scalar=bias[:, B3 + half, a : a + 1],
+                    in1=base[:, half, :],
+                    op0=ADD,
+                    op1=ADD,
+                )
+
+        def turn_back(a, source, spare):
             for part in range(2):
-                if part == 0:
+                if part == 0 or not spare:
                     t = psum_t.tile([P, 2, S], F32, name="turned")
                 else:
-                    t = psum_sum.tile([P, 2, S], F32, name="sum_%d" % (n % 2))
+                    t = psum_sum.tile([P, 2, S], F32, name="sum_%d" % (a % 2))
                 turned_x[a, part] = t
                 for i in range(2):
                     tok = slice((2 * part + i) * P, (2 * part + i + 1) * P)
                     for half in range(S_HALVES):
                         nc.tensor.transpose(t[:, i, half * P : (half + 1) * P], source[:, half, tok], ident_f32[:])
 
-        def finish(a):
+        def copy_out(a):
+            for part in range(2):
+                nc.scalar.copy(
+                    out=out_slot(a)[:, 2 * part : 2 * part + 2, a % 2, :], in_=turned_x[a, part][:]
+                )
+
+        def add_base_rows(engine_add, a):
             o = out_slot(a)
             for part in range(2):
-                if a < ROW_FIRST:
-                    nc.scalar.copy(out=o[:, 2 * part : 2 * part + 2, a % 2, :], in_=turned_x[a, part][:])
-                else:
-                    for i in (2 * part, 2 * part + 1):
-                        nc.gpsimd.tensor_tensor(
-                            out=o[:, i, a % 2, :], in0=o[:, i, a % 2, :], in1=base_rows[:, i, :], op=ADD
-                        )
+                i = slice(2 * part, 2 * part + 2)
+                engine_add(out=o[:, i, a % 2, :], in0=o[:, i, a % 2, :], in1=base_rows[:, i, :], op=ADD)
 
         nc.scalar.dma_start(out=scale[:, 0:F], in_=h1_scale.rearrange("o q k -> (o q k)").partition_broadcast(P))
-        load_w2(0)
-        load_h(0)
-        load_h(1)
         load_w3(0)
+        nc.sync.dma_start(out=v2_raw[:], in_=V2_words[0])
+        load_h(0)
+        load_w2(0)
+        nc.vector.memset(v2_raw_s[:].bitcast(I32), 0)
+        for r in range(4):
+            nc.sync.dma_start(out=v2_raw_s[r:P:32, :].bitcast(I32), in_=V2_scales[0, r:16:4, :].bitcast(I32))
+        load_h(1)
         nc.vector.memset(rows[:].bitcast(I32), 0)
         make_identity(nc, ident_f32[:])
         nc.vector.tensor_copy(out=ident_bf16[:], in_=ident_f32[:])
@@ -364,15 +355,15 @@ def tile_psicritic_pa_w4_kernel(
         nc.scalar.dma_start(out=rows[0:A, F : F + S], in_=b3)
         nc.scalar.dma_start(out=rows[A : A + 1, 0:F], in_=c2.unsqueeze(0))
         nc.scalar.dma_start(out=rows[A : A + 1, F : F + S], in_=c3.unsqueeze(0))
-        nc.vector.memset(v2_raw_s[:].bitcast(I32), 0)
         nc.vector.memset(v3_s[:].bitcast(I32), 0)
         load_w2(1)
         load_w3(1)
         load(2)
 
-        group_w2(nc.vector.tensor_copy, 0, 0, HEAD_VECTOR)
+        group_w3(0)
+        permute_v2()
         nc.scalar.copy(out=scale[:, F : 2 * F], in_=scale[:, 0:F])
-        group_w2(nc.scalar.copy, 0, HEAD_VECTOR, P)
+        group_w2(nc.scalar.copy, 0, 0, P)
         widen(0, 0)
         turn(0, 0)
         widen(0, 1)
@@ -386,8 +377,6 @@ def tile_psicritic_pa_w4_kernel(
             )
         gather(0, 0)
         gather(0, 1)
-        spread_w3(0)
-        group_w3(0)
 
         for pos, a in enumerate(ORDER):
             before = ORDER[pos - 1] if pos > 0 else None
@@ -397,29 +386,38 @@ def tile_psicritic_pa_w4_kernel(
             if pos + 3 == len(ORDER):
                 nc.sync.dma_start(
                     out=b3_rows[:].rearrange("p a s -> p (a s)"),
-                    in_=b3[ROW_FIRST:A, :].rearrange("a s -> (a s)").partition_broadcast(P),
+                    in_=b3[ROW_FIRST : ROW_FIRST + ROW_COUNT, :].rearrange("a s -> (a s)").partition_broadcast(P),
                 )
             if before is not None:
                 relu(before)
-                group_w3(a)
                 if pos > 1 and ORDER[pos - 2] == STATE:
                     keep_state()
+            fresh = ORDER[pos + 2] if after == STATE else after if a != STATE else None
             if after is not None:
-                widen(after, 0)
+                if fresh is not None:
+                    widen(fresh, 0)
                 turn(after, 0)
-                widen(after, 1)
+                if fresh is not None:
+                    widen(fresh, 1)
                 turn(after, 1)
-                group_w2(nc.vector.tensor_copy, after, 0, W2_VECTOR)
-                group_w2(nc.scalar.copy, after, W2_VECTOR, W2_SPLIT)
+                if fresh is not None:
+                    group_w3(fresh)
+                    group_w2(nc.scalar.copy, fresh, 0, W2_SPLIT)
                 gather(after, 0)
                 gather(after, 1)
-                group_w2(nc.scalar.copy, after, W2_SPLIT, P)
+                if fresh is not None:
+                    group_w2(nc.scalar.copy, fresh, W2_SPLIT, P)
             else:
-                for n in range(EARLY):
-                    multiply_out(OUT_ORDER[n], psum_t, "turned")
-                    combine(OUT_ORDER[n])
-            if after == STATE:
-                permute_v2()
+                multiply_out(BY_VECTOR[0], psum_t, "turned")
+                multiply_out(BY_SCALAR[0], psum_m, "products")
+                add_b3_rows(BY_VECTOR[0])
+                add_b3_columns(BY_SCALAR[0])
+                multiply_out(BY_VECTOR[1], psum_t, "turned")
+                multiply_out(BY_SCALAR[1], psum_m, "products")
+                add_b3_rows(BY_VECTOR[1])
+                turn_back(BY_SCALAR[0], xs[BY_SCALAR[0]], False)
+                add_b3_columns(BY_SCALAR[1])
+                copy_out(BY_SCALAR[0])
             if before is not None:
                 group_h2(before)
             quantize_h(a)
@@ -429,8 +427,6 @@ def tile_psicritic_pa_w4_kernel(
             if before is not None:
                 quantize_h2(before)
                 add_to_sums(before)
-            if after is not None:
-                spread_w3(after)
             if pos == 0:
                 nc.vector.tensor_copy(out=bias[:], in_=turned_rows[:, :, 0:32])
                 nc.vector.tensor_reduce(out=b3_sum[:], in_=bias[:, B3 : B3 + S_HALVES, 0:A], op=ADD, axis=AXIS_X)
@@ -446,30 +442,41 @@ def tile_psicritic_pa_w4_kernel(
 
         last = A - 1
         relu(last)
+        turn_back(BY_SCALAR[1], xs[BY_SCALAR[1]], False)
+        multiply_out(BY_SCALAR[2], psum_m, "products")
         group_h2(last)
         quantize_h2(last)
-        multiply_out(OUT_ORDER[EARLY], psum_t, "turned")
-        combine(OUT_ORDER[EARLY])
-        for a in OUT_ORDER[EARLY + 1 : EARLY + 3]:
-            multiply_out(a, psum_m, "products")
+        add_b3_columns(BY_SCALAR[2])
+        copy_out(BY_SCALAR[1])
+        multiply_out(LATE[0], psum_m, "products")
         add_to_sums(last)
         for half in range(S_HALVES):
             nc.vector.scalar_tensor_tensor(
                 out=base[:, half, :], in0=sums[half][:], scalar=-1.0 / A, in1=state[:, half, :], op0=MULT, op1=ADD
             )
-        turn_back("base", base, 0)
+        turn_back(BY_SCALAR[2], xs[BY_SCALAR[2]], False)
+        copy_out(BY_SCALAR[2])
+        multiply_out(LATE[1], psum_m, "products")
+        turned_x_base = []
         for part in range(2):
-            nc.scalar.copy(out=base_rows[:, 2 * part : 2 * part + 2, :], in_=turned_x["base", part][:])
-        for a in OUT_ORDER[: EARLY + 1]:
-            finish(a)
-        for n in range(EARLY + 1, A):
-            a = OUT_ORDER[n]
+            t = psum_sum.tile([P, 2, S], F32, name="sum_%d" % part)
+            turned_x_base.append(t)
+            for i in range(2):
+                tok = slice((2 * part + i) * P, (2 * part + i + 1) * P)
+                for half in range(S_HALVES):
+                    nc.tensor.transpose(t[:, i, half * P : (half + 1) * P], base[:, half, tok], ident_f32[:])
+        for part in range(2):
+            nc.scalar.copy(out=base_rows[:, 2 * part : 2 * part + 2, :], in_=turned_x_base[part][:])
+        for a in BY_VECTOR:
+            add_base_rows(nc.gpsimd.tensor_tensor, a)
+        for n, a in enumerate(LATE):
             combine(a)
-            if a < ROW_FIRST:
-                turn_back(a, xs[a], n)
-            if n + 2 < A:
-                multiply_out(OUT_ORDER[n + 2], psum_m, "products")
-            finish(a)
-            for pair in STORES_AFTER.get(a, ()):
+            turn_back(a, xs[a], True)
+            if n + 2 < len(LATE):
+                multiply_out(LATE[n + 2], psum_m, "products")
+            copy_out(a)
+            if n in (1, 2, 3):
+                add_base_rows(nc.vector.tensor_tensor, {1: 8, 2: 9, 3: 10}[n])
+            for pair in {1: [0], 2: [4], 3: [5], 4: [1, 6], 6: [2], 8: [3], 10: [7]}.get(n, ()):
                 store(2 * pair, 0)
                 store(2 * pair, 2)

@@ -35,6 +35,8 @@ ROW_FIRST, ROW_COUNT = 12, 2
 BY_VECTOR = [12, 13]
 BY_SCALAR = [8, 9, 10]
 LATE = [0, 1, 11, 2, 3, 4, 5, 6, 7, 14, 15]
+ADD_AFTER = {1: [10, 12, 13, 8, 9]}
+STORE_AFTER = {1: [0], 3: [5], 4: [1], 6: [2, 6], 8: [3, 4], 10: [7]}
 
 
 def tile_psicritic_pa_w4_kernel(
@@ -45,7 +47,7 @@ def tile_psicritic_pa_w4_kernel(
         keep = ctx.enter_context(tc.tile_pool(name="keep", bufs=1))
         loads = ctx.enter_context(tc.tile_pool(name="loads", bufs=3))
         work = ctx.enter_context(tc.tile_pool(name="work", bufs=2))
-        outs = ctx.enter_context(tc.tile_pool(name="outs", bufs=7))
+        outs = ctx.enter_context(tc.tile_pool(name="outs", bufs=8))
         psum_sum = ctx.enter_context(tc.psum_pool(name="psum_sum", bufs=1))
         psum_t = ctx.enter_context(tc.psum_pool(name="psum_t", bufs=2))
         psum_m = ctx.enter_context(tc.psum_pool(name="psum_m", bufs=4))
@@ -67,8 +69,6 @@ def tile_psicritic_pa_w4_kernel(
         b3_sum = keep.tile([P, S_HALVES], F32, name="b3_sum", align_bytes=64)
         c3_mean = keep.tile([P, S_HALVES], F32, name="c3_mean", align_bytes=64)
         state = keep.tile([P, S_HALVES, B], F32, name="state", align_bytes=64)
-        base = keep.tile([P, S_HALVES, B], F32, name="base", align_bytes=64)
-        base_rows = keep.tile([P, TOK_TILES, S], F32, name="base_rows", align_bytes=64)
 
         hb, w2r, w3r, hs, hps, hg, hq, w2g, w2q, w3p, w3g, w3q = {}, {}, {}, {}, {}, {}, {}, {}, {}, {}, {}, {}
         pm, hp, h2g, h2q, sums = {}, {}, {}, {}, {}
@@ -333,11 +333,13 @@ def tile_psicritic_pa_w4_kernel(
                     out=out_slot(a)[:, 2 * part : 2 * part + 2, a % 2, :], in_=turned_x[a, part][:]
                 )
 
-        def add_base_rows(engine_add, a):
+        def add_base_rows(a):
             o = out_slot(a)
             for part in range(2):
                 i = slice(2 * part, 2 * part + 2)
-                engine_add(out=o[:, i, a % 2, :], in0=o[:, i, a % 2, :], in1=base_rows[:, i, :], op=ADD)
+                nc.gpsimd.tensor_tensor(
+                    out=o[:, i, a % 2, :], in0=o[:, i, a % 2, :], in1=base_rows[:, i, :], op=ADD
+                )
 
         nc.scalar.dma_start(out=scale[:, 0:F], in_=h1_scale.rearrange("o q k -> (o q k)").partition_broadcast(P))
         load_w3(0)
@@ -440,6 +442,9 @@ def tile_psicritic_pa_w4_kernel(
                     op1=ADD,
                 )
 
+        base = keep.tile([P, S_HALVES, B], F32, name="scale", align_bytes=64)
+        base_rows = keep.tile([P, TOK_TILES, S], F32, name="g1_rows", align_bytes=64)
+
         last = A - 1
         relu(last)
         turn_back(BY_SCALAR[1], xs[BY_SCALAR[1]], False)
@@ -457,26 +462,25 @@ def tile_psicritic_pa_w4_kernel(
         turn_back(BY_SCALAR[2], xs[BY_SCALAR[2]], False)
         copy_out(BY_SCALAR[2])
         multiply_out(LATE[1], psum_m, "products")
-        turned_x_base = []
-        for part in range(2):
-            t = psum_sum.tile([P, 2, S], F32, name="sum_%d" % part)
-            turned_x_base.append(t)
-            for i in range(2):
-                tok = slice((2 * part + i) * P, (2 * part + i + 1) * P)
-                for half in range(S_HALVES):
-                    nc.tensor.transpose(t[:, i, half * P : (half + 1) * P], base[:, half, tok], ident_f32[:])
-        for part in range(2):
-            nc.scalar.copy(out=base_rows[:, 2 * part : 2 * part + 2, :], in_=turned_x_base[part][:])
-        for a in BY_VECTOR:
-            add_base_rows(nc.gpsimd.tensor_tensor, a)
+        def turn_base():
+            for part in range(2):
+                t = psum_t.tile([P, 2, S], F32, name="turned")
+                for i in range(2):
+                    tok = slice((2 * part + i) * P, (2 * part + i + 1) * P)
+                    for half in range(S_HALVES):
+                        nc.tensor.transpose(t[:, i, half * P : (half + 1) * P], base[:, half, tok], ident_f32[:])
+                nc.scalar.copy(out=base_rows[:, 2 * part : 2 * part + 2, :], in_=t[:])
+
         for n, a in enumerate(LATE):
             combine(a)
             turn_back(a, xs[a], True)
             if n + 2 < len(LATE):
                 multiply_out(LATE[n + 2], psum_m, "products")
             copy_out(a)
-            if n in (1, 2, 3):
-                add_base_rows(nc.vector.tensor_tensor, {1: 8, 2: 9, 3: 10}[n])
-            for pair in {1: [0], 2: [4], 3: [5], 4: [1, 6], 6: [2], 8: [3], 10: [7]}.get(n, ()):
+            if n == 1:
+                turn_base()
+            for early in ADD_AFTER.get(n, ()):
+                add_base_rows(early)
+            for pair in STORE_AFTER.get(n, ()):
                 store(2 * pair, 0)
                 store(2 * pair, 2)

from contextlib import ExitStack

import concourse.mybir as mybir
from concourse.masks import make_identity

B, A, S, F = 512, 16, 256, 512
FLOPS = 2 * B * (A + 1) * (F * F + F * S)

P = 128
PACK = 4
TOK_TILES = B // P
S_HALVES = S // P

F32 = mybir.dt.float32
BF16 = mybir.dt.bfloat16
I32 = mybir.dt.int32
U32 = mybir.dt.uint32
U8 = mybir.dt.uint8
FP8 = mybir.dt.float8_e4m3fn
E4M3X4 = mybir.dt.float8_e4m3fn_x4
E2M1X4 = mybir.dt.float4_e2m1fn_x4
ADD = mybir.AluOpType.add
MULT = mybir.AluOpType.mult
MAX = mybir.AluOpType.max
RELU = mybir.ActivationFunctionType.Relu
IDENTITY = mybir.ActivationFunctionType.Identity
AXIS_X = mybir.AxisListType.X

STATE = A
ORDER = list(range(5)) + [STATE] + list(range(5, A))
SHARED_RELU = (ORDER[ORDER.index(STATE) - 1], ORDER[-1])
B2, B3 = 0, 4
W2_SPLIT = 64
ROW_FIRST, ROW_COUNT = 12, 2
BY_VECTOR = [12, 13]
BY_SCALAR = [8, 9, 10]
LATE = [0, 1, 11, 2, 3, 4, 5, 6, 7, 14, 15]
ADD_AFTER = {1: [10, 12, 13, 8, 9]}
STORE_AFTER = {1: [0], 3: [5], 4: [1], 6: [2, 6], 8: [3, 4], 10: [7]}


def tile_psicritic_pa_w4_kernel(
    tc, h1_bytes, h1_scale, W2, b2, W3, b3, g1, V2_words, V2_scales, c2, V3_words, V3_scales, c3, out
):
    nc = tc.nc
    with ExitStack() as ctx:
        keep = ctx.enter_context(tc.tile_pool(name="keep", bufs=1))
        loads = ctx.enter_context(tc.tile_pool(name="loads", bufs=3))
        work = ctx.enter_context(tc.tile_pool(name="work", bufs=2))
        outs = ctx.enter_context(tc.tile_pool(name="outs", bufs=8))
        psum_sum = ctx.enter_context(tc.psum_pool(name="psum_sum", bufs=1))
        psum_t = ctx.enter_context(tc.psum_pool(name="psum_t", bufs=2))
        psum_m = ctx.enter_context(tc.psum_pool(name="psum_m", bufs=4))
        ctx.enter_context(tc.manual_schedule())

        rows = keep.tile([P, F + S], BF16, name="rows", align_bytes=64)
        v2_raw_s = keep.tile([P, F], U8, name="v2_raw_s", align_bytes=64)
        v3_s = keep.tile([P, S], U8, name="v3_s", align_bytes=64)
        v2_raw = keep.tile([P, 2 * F], U8, name="v2_raw", align_bytes=64)
        v3_w = keep.tile([P, 2 * S], U8, name="v3_w", align_bytes=64)
        v2_w = keep.tile([P, 2 * F], U8, name="v2_w", align_bytes=64)
        v2_s = keep.tile([P, F], U8, name="v2_s", align_bytes=64)
        scale = keep.tile([P, 2 * F], F32, name="scale", align_bytes=64)
        ident_f32 = keep.tile([P, P], F32, name="ident_f32", align_bytes=64)
        ident_bf16 = keep.tile([P, P], BF16, name="ident_bf16", align_bytes=64)
        g1_rows = keep.tile([P, TOK_TILES, F], BF16, name="g1_rows", align_bytes=64)
        b3_rows = keep.tile([P, ROW_COUNT, S], BF16, name="b3_rows", align_bytes=64)
        bias = keep.tile([P, 6, 32], F32, name="bias", align_bytes=64)
        b3_sum = keep.tile([P, S_HALVES], F32, name="b3_sum", align_bytes=64)
        c3_mean = keep.tile([P, S_HALVES], F32, name="c3_mean", align_bytes=64)
        state = keep.tile([P, S_HALVES, B], F32, name="state", align_bytes=64)

        hb, w2r, w3r, hs, hps, hg, hq, w2g, w2q, w3p, w3g, w3q = {}, {}, {}, {}, {}, {}, {}, {}, {}, {}, {}, {}
        pm, hp, h2g, h2q, sums = {}, {}, {}, {}, {}

        def load_h(a):
            hb[a] = loads.tile([P, TOK_TILES, F], U8, name="h_bytes", align_bytes=64)
            nc.sync.dma_start(out=hb[a][:], in_=h1_bytes[:, a, :].rearrange("(i p) k -> p i k", p=P))

        def load_w2(a):
            w2r[a] = loads.tile([P, PACK, F], BF16, name="w2_rows", align_bytes=64)
            nc.sync.dma_start(out=w2r[a][:], in_=W2[a].rearrange("(p j) n -> p j n", j=PACK))

        def load_w3(a):
            w3r[a] = loads.tile([P, PACK, S], BF16, name="w3_rows", align_bytes=64)
            nc.sync.dma_start(out=w3r[a][:], in_=W3[a].rearrange("(p j) n -> p j n", j=PACK))

        def load_state():
            nc.sync.dma_start(out=g1_rows[:], in_=g1.rearrange("(i p) k -> p i k", p=P))
            nc.sync.dma_start(out=v3_w[:], in_=V3_words[0])
            for r in range(4):
                nc.sync.dma_start(out=v3_s[r:P:32, :].bitcast(I32), in_=V3_scales[0, r:16:4, :].bitcast(I32))
            hs[STATE] = g1_rows

        def load(a):
            if a == STATE:
                load_state()
            else:
                load_h(a)
                load_w2(a)
                load_w3(a)

        def widen(a, half):
            if half == 0:
                hs[a] = work.tile([P, TOK_TILES, F], BF16, name="h_rows", align_bytes=64)
            i = slice(2 * half, 2 * half + 2)
            nc.vector.tensor_tensor(
                out=hs[a][:, i, :].rearrange("p i k -> p (i k)"),
                in0=hb[a][:, i, :].rearrange("p i k -> p (i k)").bitcast(FP8),
                in1=scale[:],
                op=MULT,
            )

        def turn(a, half):
            hps[a, half] = psum_t.tile([P, 2, 2, P], F32, name="turned")
            for i in range(2):
                words = hs[a][:, 2 * half + i, :].bitcast(F32)
                for u in range(2):
                    nc.tensor.transpose(hps[a, half][:, i, u, :], words[:, u::2], ident_f32[:])

        def gather(a, half):
            if half == 0:
                hg[a] = work.tile([P, B * PACK], BF16, name="h_grouped", align_bytes=64)
            n = B * PACK // 2
            nc.scalar.copy(
                out=hg[a][:, half * n : (half + 1) * n].bitcast(F32).rearrange("p (i r u) -> p i r u", i=2, u=2),
                in_=hps[a, half][:].rearrange("p i u r -> p i r u"),
            )

        def quantize(pool, name, grouped, width):
            codes = pool.tile([P, width], U32, name=name + "_codes", align_bytes=64)
            scales = pool.tile([P, width], U8, name=name + "_scales", align_bytes=64)
            nc.vector.quantize_mx(out=codes[:].bitcast(E4M3X4), scales=scales[:], in_=grouped[:])
            return codes, scales

        def quantize_h(a):
            hq[a] = quantize(work, "h", hg[a], B)

        def group_w2(engine_copy, a, first, last):
            if a == STATE:
                return
            if a not in w2g:
                w2g[a] = work.tile([P, F * PACK], BF16, name="w2_grouped", align_bytes=64)
            m = slice(first, last)
            engine_copy(
                out=w2g[a][:].rearrange("p (t m j) -> p m j t", t=PACK, j=PACK)[:, m],
                in_=w2r[a][:].rearrange("p j (m t) -> p m j t", t=PACK)[:, m],
            )

        def quantize_w2(a):
            if a != STATE:
                w2q[a] = quantize(work, "w2", w2g[a], F)

        def group_w3(a):
            if a == STATE:
                return
            w3g[a] = work.tile([P, S * PACK], BF16, name="w3_grouped", align_bytes=64)
            nc.vector.tensor_copy(
                out=w3g[a][:].rearrange("p (c i j) -> p c j i", i=4, j=PACK),
                in_=w3r[a][:].rearrange("p j (c i) -> p c j i", i=4),
            )

        def quantize_w3(a):
            if a != STATE:
                w3q[a] = quantize(keep, "w3_%d" % a, w3g[a], S)

        def permute_v2():
            nc.vector.tensor_copy(
                out=v2_w[:].rearrange("p (t m b) -> p m t b", t=PACK, b=2),
                in_=v2_raw[:].rearrange("p (m t b) -> p m t b", t=PACK, b=2),
            )
            nc.vector.tensor_copy(
                out=v2_s[:].rearrange("p (t m) -> p m t", t=PACK),
                in_=v2_raw_s[:].rearrange("p (m t) -> p m t", t=PACK),
            )

        def multiply1(a):
            for t in range(PACK):
                pm[a, t] = psum_m.tile([P, B], F32, name="products")
                cols = slice(t * P, (t + 1) * P)
                if a == STATE:
                    lhsT = v2_w[:, 2 * t * P : 2 * (t + 1) * P].bitcast(E2M1X4)
                    lhsT_scale = v2_s[:, cols]
                else:
                    lhsT = w2q[a][0][:, cols].bitcast(E4M3X4)
                    lhsT_scale = w2q[a][1][:, cols]
                nc.tensor.matmul_mx(
                    out=pm[a, t][:],
                    lhsT=lhsT,
                    lhsT_scale=lhsT_scale,
                    rhs=hq[a][0][:].bitcast(E4M3X4),
                    rhs_scale=hq[a][1][:],
                    start=True,
                    stop=True,
                )

        def relu(a):
            hp[a] = work.tile([P, PACK, B], BF16, name="h2_planes", align_bytes=64)
            for t in range(PACK):
                column = bias[:, B2 + t, a : a + 1]
                if a in SHARED_RELU and t % 2 == 1:
                    nc.vector.tensor_scalar(
                        out=hp[a][:, t, :], in0=pm[a, t][:], scalar1=column, scalar2=0.0, op0=ADD, op1=MAX
                    )
                else:
                    nc.scalar.activation(out=hp[a][:, t, :], in_=pm[a, t][:], func=RELU, bias=column)

        def group_h2(a):
            h2g[a] = work.tile([P, B * PACK], BF16, name="h2_grouped", align_bytes=64)
            nc.vector.tensor_copy(
                out=h2g[a][:].rearrange("p (c i t) -> p c t i", i=4, t=PACK),
                in_=hp[a][:].rearrange("p t (c i) -> p c t i", i=4),
            )

        def quantize_h2(a):
            h2q[a] = quantize(keep, "h2_%d" % a, h2g[a], B)

        def multiply2(a, out_tile, half, start, stop):
            cols = slice(half * P, (half + 1) * P)
            if a == STATE:
                lhsT = v3_w[:, 2 * half * P : 2 * (half + 1) * P].bitcast(E2M1X4)
                lhsT_scale = v3_s[:, cols]
            else:
                lhsT = w3q[a][0][:, cols].bitcast(E4M3X4)
                lhsT_scale = w3q[a][1][:, cols]
            nc.tensor.matmul_mx(
                out=out_tile[:],
                lhsT=lhsT,
                lhsT_scale=lhsT_scale,
                rhs=h2q[a][0][:].bitcast(E4M3X4),
                rhs_scale=h2q[a][1][:],
                start=start,
                stop=stop,
            )

        def add_to_sums(a):
            for half in range(S_HALVES):
                if a == STATE:
                    pm[a, "out", half] = psum_m.tile([P, B], F32, name="products")
                    multiply2(a, pm[a, "out", half], half, True, True)
                else:
                    if a == 0:
                        sums[half] = psum_sum.tile([P, B], F32, name="sum_%d" % half)
                    multiply2(a, sums[half], half, a == 0, a == A - 1)

        def keep_state():
            for half in range(S_HALVES):
                nc.scalar.activation(
                    out=state[:, half, :],
                    in_=pm[STATE, "out", half][:],
                    func=IDENTITY,
                    bias=c3_mean[:, half : half + 1],
                )

        adv, xs, turned_x, out_rows = {}, {}, {}, {}

        def out_slot(a):
            if a // 2 not in out_rows:
                out_rows[a // 2] = outs.tile([P, TOK_TILES, 2, S], F32, name="out_rows", align_bytes=64)
            return out_rows[a // 2]

        def store(a, first):
            first, last = first, first + 2
            nc.sync.dma_start(
                out=out[first * P : last * P, a - a % 2 : a - a % 2 + 2, :].rearrange("(i p) a s -> p i (a s)", p=P),
                in_=out_slot(a)[:, first:last].rearrange("p i a s -> p i (a s)"),
            )

        def multiply_out(a, pool, name):
            for part in range(2):
                adv[a, part] = pool.tile([P, B], F32, name=name)
                if a not in BY_VECTOR:
                    multiply2(a, adv[a, part], part, True, True)
                else:
                    for i in range(2):
                        tok = slice((2 * part + i) * P, (2 * part + i + 1) * P)
                        nc.tensor.matmul_mx(
                            out=adv[a, part][:, i * S : (i + 1) * S],
                            lhsT=h2q[a][0][:, tok].bitcast(E4M3X4),
                            lhsT_scale=h2q[a][1][:, tok],
                            rhs=w3q[a][0][:].bitcast(E4M3X4),
                            rhs_scale=w3q[a][1][:],
                            start=True,
                            stop=True,
                        )

        def add_b3_rows(a):
            for i in range(TOK_TILES):
                nc.vector.tensor_tensor(
                    out=out_slot(a)[:, i, a % 2, :],
                    in0=adv[a, i // 2][:, i % 2 * S : (i % 2 + 1) * S],
                    in1=b3_rows[:, a - ROW_FIRST, :],
                    op=ADD,
                )

        def add_b3_columns(a):
            xs[a] = work.tile([P, S_HALVES, B], F32, name="combined", align_bytes=64)
            for half in range(S_HALVES):
                nc.scalar.activation(
                    out=xs[a][:, half, :],
                    in_=adv[a, half][:],
                    func=IDENTITY,
                    bias=bias[:, B3 + half, a : a + 1],
                )

        def combine(a):
            xs[a] = work.tile([P, S_HALVES, B], F32, name="combined", align_bytes=64)
            for half in range(S_HALVES):
                nc.vector.scalar_tensor_tensor(
                    out=xs[a][:, half, :],
                    in0=adv[a, half][:],
                    scalar=bias[:, B3 + half, a : a + 1],
                    in1=base[:, half, :],
                    op0=ADD,
                    op1=ADD,
                )

        def turn_back(a, source, spare):
            for part in range(2):
                if part == 0 or not spare:
                    t = psum_t.tile([P, 2, S], F32, name="turned")
                else:
                    t = psum_sum.tile([P, 2, S], F32, name="sum_%d" % (a % 2))
                turned_x[a, part] = t
                for i in range(2):
                    tok = slice((2 * part + i) * P, (2 * part + i + 1) * P)
                    for half in range(S_HALVES):
                        nc.tensor.transpose(t[:, i, half * P : (half + 1) * P], source[:, half, tok], ident_f32[:])

        def copy_out(a):
            for part in range(2):
                nc.scalar.copy(
                    out=out_slot(a)[:, 2 * part : 2 * part + 2, a % 2, :], in_=turned_x[a, part][:]
                )

        def add_base_rows(a):
            o = out_slot(a)
            for part in range(2):
                i = slice(2 * part, 2 * part + 2)
                nc.gpsimd.tensor_tensor(
                    out=o[:, i, a % 2, :], in0=o[:, i, a % 2, :], in1=base_rows[:, i, :], op=ADD
                )

        nc.scalar.dma_start(out=scale[:, 0:F], in_=h1_scale.rearrange("o q k -> (o q k)").partition_broadcast(P))
        load_w3(0)
        nc.sync.dma_start(out=v2_raw[:], in_=V2_words[0])
        load_h(0)
        load_w2(0)
        nc.vector.memset(v2_raw_s[:].bitcast(I32), 0)
        for r in range(4):
            nc.sync.dma_start(out=v2_raw_s[r:P:32, :].bitcast(I32), in_=V2_scales[0, r:16:4, :].bitcast(I32))
        load_h(1)
        nc.vector.memset(rows[:].bitcast(I32), 0)
        make_identity(nc, ident_f32[:])
        nc.vector.tensor_copy(out=ident_bf16[:], in_=ident_f32[:])
        nc.scalar.dma_start(out=rows[0:A, 0:F], in_=b2)
        nc.scalar.dma_start(out=rows[0:A, F : F + S], in_=b3)
        nc.scalar.dma_start(out=rows[A : A + 1, 0:F], in_=c2.unsqueeze(0))
        nc.scalar.dma_start(out=rows[A : A + 1, F : F + S], in_=c3.unsqueeze(0))
        nc.vector.memset(v3_s[:].bitcast(I32), 0)
        load_w2(1)
        load_w3(1)
        load(2)

        group_w3(0)
        permute_v2()
        nc.scalar.copy(out=scale[:, F : 2 * F], in_=scale[:, 0:F])
        group_w2(nc.scalar.copy, 0, 0, P)
        widen(0, 0)
        turn(0, 0)
        widen(0, 1)
        turn(0, 1)
        turned_rows = psum_m.tile([P, 6, P], BF16, name="products")
        for t in range(PACK):
            nc.tensor.transpose(turned_rows[:, B2 + t, :], rows[:, t:F:PACK], ident_bf16[:])
        for half in range(S_HALVES):
            nc.tensor.transpose(
                turned_rows[:, B3 + half, :], rows[:, F + half * P : F + (half + 1) * P], ident_bf16[:]
            )
        gather(0, 0)
        gather(0, 1)

        for pos, a in enumerate(ORDER):
            before = ORDER[pos - 1] if pos > 0 else None
            after = ORDER[pos + 1] if pos + 1 < len(ORDER) else None
            if pos + 3 < len(ORDER):
                load(ORDER[pos + 3])
            if pos + 3 == len(ORDER):
                nc.sync.dma_start(
                    out=b3_rows[:].rearrange("p a s -> p (a s)"),
                    in_=b3[ROW_FIRST : ROW_FIRST + ROW_COUNT, :].rearrange("a s -> (a s)").partition_broadcast(P),
                )
            if before is not None:
                relu(before)
                if pos > 1 and ORDER[pos - 2] == STATE:
                    keep_state()
            fresh = ORDER[pos + 2] if after == STATE else after if a != STATE else None
            if after is not None:
                if fresh is not None:
                    widen(fresh, 0)
                turn(after, 0)
                if fresh is not None:
                    widen(fresh, 1)
                turn(after, 1)
                if fresh is not None:
                    group_w3(fresh)
                    group_w2(nc.scalar.copy, fresh, 0, W2_SPLIT)
                gather(after, 0)
                gather(after, 1)
                if fresh is not None:
                    group_w2(nc.scalar.copy, fresh, W2_SPLIT, P)
            else:
                multiply_out(BY_VECTOR[0], psum_t, "turned")
                multiply_out(BY_SCALAR[0], psum_m, "products")
                add_b3_rows(BY_VECTOR[0])
                add_b3_columns(BY_SCALAR[0])
                multiply_out(BY_VECTOR[1], psum_t, "turned")
                multiply_out(BY_SCALAR[1], psum_m, "products")
                add_b3_rows(BY_VECTOR[1])
                turn_back(BY_SCALAR[0], xs[BY_SCALAR[0]], False)
                add_b3_columns(BY_SCALAR[1])
                copy_out(BY_SCALAR[0])
            if before is not None:
                group_h2(before)
            quantize_h(a)
            quantize_w2(a)
            multiply1(a)
            quantize_w3(a)
            if before is not None:
                quantize_h2(before)
                add_to_sums(before)
            if pos == 0:
                nc.vector.tensor_copy(out=bias[:], in_=turned_rows[:, :, 0:32])
                nc.vector.tensor_reduce(out=b3_sum[:], in_=bias[:, B3 : B3 + S_HALVES, 0:A], op=ADD, axis=AXIS_X)
            if pos == 1:
                nc.vector.scalar_tensor_tensor(
                    out=c3_mean[:],
                    in0=b3_sum[:],
                    scalar=-1.0 / A,
                    in1=bias[:, B3 : B3 + S_HALVES, A],
                    op0=MULT,
                    op1=ADD,
                )

        base = keep.tile([P, S_HALVES, B], F32, name="scale", align_bytes=64)
        base_rows = keep.tile([P, TOK_TILES, S], F32, name="g1_rows", align_bytes=64)

        last = A - 1
        relu(last)
        turn_back(BY_SCALAR[1], xs[BY_SCALAR[1]], False)
        multiply_out(BY_SCALAR[2], psum_m, "products")
        group_h2(last)
        quantize_h2(last)
        add_b3_columns(BY_SCALAR[2])
        copy_out(BY_SCALAR[1])
        multiply_out(LATE[0], psum_m, "products")
        add_to_sums(last)
        for half in range(S_HALVES):
            nc.vector.scalar_tensor_tensor(
                out=base[:, half, :], in0=sums[half][:], scalar=-1.0 / A, in1=state[:, half, :], op0=MULT, op1=ADD
            )
        turn_back(BY_SCALAR[2], xs[BY_SCALAR[2]], False)
        copy_out(BY_SCALAR[2])
        multiply_out(LATE[1], psum_m, "products")
        def turn_base():
            for part in range(2):
                t = psum_t.tile([P, 2, S], F32, name="turned")
                for i in range(2):
                    tok = slice((2 * part + i) * P, (2 * part + i + 1) * P)
                    for half in range(S_HALVES):
                        nc.tensor.transpose(t[:, i, half * P : (half + 1) * P], base[:, half, tok], ident_f32[:])
                nc.scalar.copy(out=base_rows[:, 2 * part : 2 * part + 2, :], in_=t[:])

        for n, a in enumerate(LATE):
            combine(a)
            turn_back(a, xs[a], True)
            if n + 2 < len(LATE):
                multiply_out(LATE[n + 2], psum_m, "products")
            copy_out(a)
            if n == 1:
                turn_base()
            for early in ADD_AFTER.get(n, ()):
                add_base_rows(early)
            for pair in STORE_AFTER.get(n, ()):
                store(2 * pair, 0)
                store(2 * pair, 2)
